import numpy as np
import ml_dtypes

BF16 = ml_dtypes.bfloat16


def bf(x):
    return np.asarray(x, np.float32).astype(BF16)


def f32(x):
    return np.asarray(x, np.float32)


def f64(x):
    return np.asarray(x).astype(np.float64)


def striped(idx):
    return np.tile(idx.reshape(-1, 16).T, (8, 1))


L, S, M, N = 512, 256, 256, 512


def silu(v):
    return v / (1.0 + np.exp(-v))


def setup_inputs():
    return {
        "table": f32(np.random.standard_normal((L, S))),
        "emb_w": bf(np.random.standard_normal((L, L)) / np.sqrt(L)),
        "emb_b": f32(0.1 * np.random.standard_normal((L, 1))),
        "cond_w2": bf(np.random.standard_normal((L, M)) / np.sqrt(L)),
        "cond_b2": f32(0.1 * np.random.standard_normal((M, 1))),
        "mlp_b2": f32(np.random.standard_normal((M, 1))),
        "x": f32(np.random.standard_normal((M, N))),
        "offs": striped(np.random.permutation(np.tile(np.arange(S), 2))[:N]),
    }


def reference(table, emb_w, emb_b, cond_w2, cond_b2, mlp_b2, x, offs):
    idx = offs[:16].T.reshape(-1)
    t0 = np.concatenate([np.zeros(L // 2), np.ones(L // 2)])[:, None]
    e = silu(f64(table)[:, idx])
    cond = f64(emb_w).T @ e + f64(emb_b) + t0
    scale2 = f64(cond_w2).T @ silu(cond) + f64(cond_b2)
    return f64(x) + f64(mlp_b2) * (1.0 + scale2)

@@ -1,0 +1,102 @@
+import concourse.mybir as mybir
+
+F32 = mybir.dt.float32
+BF16 = mybir.dt.bfloat16
+U16 = mybir.dt.uint16
+COPY = mybir.ActivationFunctionType.Copy
+SILU = mybir.ActivationFunctionType.Silu
+ADD = mybir.AluOpType.add
+MULT = mybir.AluOpType.mult
+
+P = 128
+L, S, M, N = 512, 256, 256, 512
+LB = L // P
+MB = M // P
+PIECE = S
+FLOPS = 2 * L * L * N + 2 * L * M * N
+
+
+def tile_conditionalflow_kernel(tc, table, emb_w, emb_b, cond_w2, cond_b2, mlp_b2, x, offs, out):
+    nc = tc.nc
+    with (
+        tc.tile_pool(name="held", bufs=1) as held,
+        tc.psum_pool(name="psum", bufs=1) as psum,
+    ):
+        offsets = held.tile([P, N // 16], U16, name="offsets")
+        nc.sync.dma_start(offsets[:], offs)
+        table_blocks = table.rearrange("(b p) s -> b p s", p=P)
+        windows = []
+        for kb in range(LB):
+            window = held.tile([P, S], F32, name=f"window{kb}")
+            nc.sync.dma_start(window[:], table_blocks[kb, :, :])
+            windows.append(window)
+
+        emb_w_blocks = emb_w.rearrange("(b p) d -> b p d", p=P)
+        emb_w_sb = []
+        for kb in range(LB):
+            weights = held.tile([P, L], BF16, name=f"emb_w{kb}")
+            nc.scalar.dma_start(weights[:], emb_w_blocks[kb, :, :])
+            emb_w_sb.append(weights)
+
+        cond_bias = held.tile([P, LB], F32, name="cond_bias")
+        branch = held.tile([P, MB], F32, name="branch")
+        scale_bias = held.tile([P, MB], F32, name="scale_bias")
+        with nc.allow_non_contiguous_dma(reason="a bias vector, one value to a partition"):
+            nc.gpsimd.dma_start(cond_bias[:], emb_b.rearrange("(b p) o -> p (b o)", p=P))
+            nc.gpsimd.dma_start(branch[:], mlp_b2.rearrange("(b p) o -> p (b o)", p=P))
+            nc.gpsimd.dma_start(scale_bias[:], cond_b2.rearrange("(b p) o -> p (b o)", p=P))
+        cond_w2_sb = held.tile([P, LB, M], BF16, name="cond_w2_sb")
+        nc.gpsimd.dma_start(cond_w2_sb[:], cond_w2.rearrange("(b p) m -> p b m", p=P))
+        x_blocks = x.rearrange("(b p) n -> b p n", p=P)
+        residual = []
+        for mb in range(MB):
+            x_sb = held.tile([P, N], F32, name=f"x{mb}")
+            nc.gpsimd.dma_start(x_sb[:], x_blocks[mb, :, :])
+            residual.append(x_sb)
+
+        nc.vector.tensor_scalar_add(cond_bias[:, LB // 2 :], cond_bias[:, LB // 2 :], 1.0)
+        shift = held.tile([P, MB], F32, name="shift")
+        nc.vector.scalar_tensor_tensor(shift[:], scale_bias[:], 1.0, branch[:], ADD, MULT)
+        for mb in range(MB):
+            nc.vector.tensor_scalar_add(residual[mb][:], residual[mb][:], shift[:, mb : mb + 1])
+
+        cond_ps = [psum.tile([P, N], F32, name=f"cond_ps{db}") for db in range(LB)]
+        for kb in range(LB):
+            picked = held.tile([P, N], F32, name=f"picked{kb}")
+            for j0 in range(0, N, PIECE):
+                nc.scalar.activation(
+                    picked[:, j0 : j0 + PIECE],
+                    windows[kb][:].indirect(offsets[:, j0 // 16 : (j0 + PIECE) // 16]),
+                    COPY,
+                )
+            e_bf = held.tile([P, N], BF16, name=f"e_bf{kb}")
+            nc.scalar.activation(e_bf[:], picked[:], SILU)
+            for db in range(LB):
+                nc.tensor.matmul(
+                    cond_ps[db][:],
+                    emb_w_sb[kb][:, db * P : (db + 1) * P],
+                    e_bf[:],
+                    start=(kb == 0),
+                    stop=(kb == LB - 1),
+                )
+
+        scale_ps = [psum.tile([P, N], F32, name=f"scale_ps{mb}") for mb in range(MB)]
+        for db in range(LB):
+            h_bf = held.tile([P, N], BF16, name=f"h_bf{db}")
+            nc.scalar.activation(h_bf[:], cond_ps[db][:], SILU, bias=cond_bias[:, db : db + 1])
+            for mb in range(MB):
+                nc.tensor.matmul(
+                    scale_ps[mb][:],
+                    cond_w2_sb[:, db, mb * P : (mb + 1) * P],
+                    h_bf[:],
+                    start=(db == 0),
+                    stop=(db == LB - 1),
+                )
+
+        out_blocks = out.rearrange("(b p) n -> b p n", p=P)
+        for mb in range(MB):
+            result = held.tile([P, N], F32, name=f"result{mb}")
+            nc.vector.scalar_tensor_tensor(
+                result[:], scale_ps[mb][:], branch[:, mb : mb + 1], residual[mb][:], MULT, ADD
+            )
+            nc.sync.dma_start(out_blocks[mb, :, :], result[:])

@@ -20,6 +20,7 @@ def tile_conditionalflow_kernel(tc, table, emb_w, emb_b, cond_w2, cond_b2, mlp_b
     nc = tc.nc
     with (
         tc.tile_pool(name="held", bufs=1) as held,
+        tc.tile_pool(name="turn", bufs=1) as turn,
         tc.psum_pool(name="psum", bufs=1) as psum,
     ):
         offsets = held.tile([P, N // 16], U16, name="offsets")
@@ -62,7 +63,7 @@ def tile_conditionalflow_kernel(tc, table, emb_w, emb_b, cond_w2, cond_b2, mlp_b
 
         cond_ps = [psum.tile([P, N], F32, name=f"cond_ps{db}") for db in range(LB)]
         for kb in range(LB):
-            picked = held.tile([P, N], F32, name=f"picked{kb}")
+            picked = turn.tile([P, N], F32, name="picked")
             for j0 in range(0, N, PIECE):
                 nc.scalar.activation(
                     picked[:, j0 : j0 + PIECE],

@@ -20,9 +20,12 @@ def tile_conditionalflow_kernel(tc, table, emb_w, emb_b, cond_w2, cond_b2, mlp_b
     nc = tc.nc
     with (
         tc.tile_pool(name="held", bufs=1) as held,
-        tc.tile_pool(name="turn", bufs=1) as turn,
         tc.psum_pool(name="psum", bufs=1) as psum,
     ):
+        scratch = held.tile([P, 1], F32, name="scratch")
+        nc.vector.memset(scratch[:], 0.0)
+        nc.scalar.activation(scratch[:], scratch[:], SILU)
+
         offsets = held.tile([P, N // 16], U16, name="offsets")
         nc.sync.dma_start(offsets[:], offs)
         table_blocks = table.rearrange("(b p) s -> b p s", p=P)
@@ -63,7 +66,7 @@ def tile_conditionalflow_kernel(tc, table, emb_w, emb_b, cond_w2, cond_b2, mlp_b
 
         cond_ps = [psum.tile([P, N], F32, name=f"cond_ps{db}") for db in range(LB)]
         for kb in range(LB):
-            picked = turn.tile([P, N], F32, name="picked")
+            picked = held.tile([P, N], F32, name=f"picked{kb}")
             for j0 in range(0, N, PIECE):
                 nc.scalar.activation(
                     picked[:, j0 : j0 + PIECE],

@@ -13,6 +13,8 @@ L, S, M, N = 512, 256, 256, 512
 LB = L // P
 MB = M // P
 PIECE = S
+PIECES = N // PIECE
+PSUM_BANKS = 8
 FLOPS = 2 * L * L * N + 2 * L * M * N
 
 
@@ -20,7 +22,7 @@ def tile_conditionalflow_kernel(tc, table, emb_w, emb_b, cond_w2, cond_b2, mlp_b
     nc = tc.nc
     with (
         tc.tile_pool(name="held", bufs=1) as held,
-        tc.psum_pool(name="psum", bufs=1) as psum,
+        tc.psum_pool(name="psum", bufs=PSUM_BANKS) as psum,
     ):
         scratch = held.tile([P, 1], F32, name="scratch")
         nc.vector.memset(scratch[:], 0.0)
@@ -34,21 +36,20 @@ def tile_conditionalflow_kernel(tc, table, emb_w, emb_b, cond_w2, cond_b2, mlp_b
             window = held.tile([P, S], F32, name=f"window{kb}")
             nc.sync.dma_start(window[:], table_blocks[kb, :, :])
             windows.append(window)
-
         emb_w_blocks = emb_w.rearrange("(b p) d -> b p d", p=P)
         emb_w_sb = []
         for kb in range(LB):
             weights = held.tile([P, L], BF16, name=f"emb_w{kb}")
-            nc.scalar.dma_start(weights[:], emb_w_blocks[kb, :, :])
+            nc.sync.dma_start(weights[:], emb_w_blocks[kb, :, :])
             emb_w_sb.append(weights)
-
         cond_bias = held.tile([P, LB], F32, name="cond_bias")
         branch = held.tile([P, MB], F32, name="branch")
         scale_bias = held.tile([P, MB], F32, name="scale_bias")
         with nc.allow_non_contiguous_dma(reason="a bias vector, one value to a partition"):
-            nc.gpsimd.dma_start(cond_bias[:], emb_b.rearrange("(b p) o -> p (b o)", p=P))
-            nc.gpsimd.dma_start(branch[:], mlp_b2.rearrange("(b p) o -> p (b o)", p=P))
-            nc.gpsimd.dma_start(scale_bias[:], cond_b2.rearrange("(b p) o -> p (b o)", p=P))
+            nc.sync.dma_start(cond_bias[:], emb_b.rearrange("(b p) o -> p (b o)", p=P))
+            nc.sync.dma_start(branch[:], mlp_b2.rearrange("(b p) o -> p (b o)", p=P))
+            nc.sync.dma_start(scale_bias[:], cond_b2.rearrange("(b p) o -> p (b o)", p=P))
+
         cond_w2_sb = held.tile([P, LB, M], BF16, name="cond_w2_sb")
         nc.gpsimd.dma_start(cond_w2_sb[:], cond_w2.rearrange("(b p) m -> p b m", p=P))
         x_blocks = x.rearrange("(b p) n -> b p n", p=P)
@@ -64,43 +65,56 @@ def tile_conditionalflow_kernel(tc, table, emb_w, emb_b, cond_w2, cond_b2, mlp_b
         for mb in range(MB):
             nc.vector.tensor_scalar_add(residual[mb][:], residual[mb][:], shift[:, mb : mb + 1])
 
-        cond_ps = [psum.tile([P, N], F32, name=f"cond_ps{db}") for db in range(LB)]
-        for kb in range(LB):
-            picked = held.tile([P, N], F32, name=f"picked{kb}")
-            for j0 in range(0, N, PIECE):
-                nc.scalar.activation(
-                    picked[:, j0 : j0 + PIECE],
-                    windows[kb][:].indirect(offsets[:, j0 // 16 : (j0 + PIECE) // 16]),
-                    COPY,
-                )
-            e_bf = held.tile([P, N], BF16, name=f"e_bf{kb}")
-            nc.scalar.activation(e_bf[:], picked[:], SILU)
-            for db in range(LB):
-                nc.tensor.matmul(
-                    cond_ps[db][:],
-                    emb_w_sb[kb][:, db * P : (db + 1) * P],
-                    e_bf[:],
-                    start=(kb == 0),
-                    stop=(kb == LB - 1),
-                )
-
-        scale_ps = [psum.tile([P, N], F32, name=f"scale_ps{mb}") for mb in range(MB)]
-        for db in range(LB):
-            h_bf = held.tile([P, N], BF16, name=f"h_bf{db}")
-            nc.scalar.activation(h_bf[:], cond_ps[db][:], SILU, bias=cond_bias[:, db : db + 1])
-            for mb in range(MB):
-                nc.tensor.matmul(
-                    scale_ps[mb][:],
-                    cond_w2_sb[:, db, mb * P : (mb + 1) * P],
-                    h_bf[:],
-                    start=(db == 0),
-                    stop=(db == LB - 1),
-                )
+        cond_ps = []
+        for piece in range(PIECES):
+            piece_offsets = offsets[:, piece * PIECE // 16 : (piece + 1) * PIECE // 16]
+            picked = []
+            for kb in range(LB):
+                columns = held.tile([P, PIECE], F32, name=f"picked{piece}_{kb}")
+                nc.scalar.activation(columns[:], windows[kb][:].indirect(piece_offsets), COPY)
+                picked.append(columns)
+            e_bf = []
+            for kb in range(LB):
+                activated = held.tile([P, PIECE], BF16, name=f"e_bf{piece}_{kb}")
+                nc.scalar.activation(activated[:], picked[kb][:], SILU)
+                e_bf.append(activated)
+            banks = [psum.tile([P, PIECE], F32, name=f"cond_ps{piece}_{db}", tag="bank") for db in range(LB)]
+            for kb in range(LB):
+                for db in range(LB):
+                    nc.tensor.matmul(
+                        banks[db][:],
+                        emb_w_sb[kb][:, db * P : (db + 1) * P],
+                        e_bf[kb][:],
+                        start=(kb == 0),
+                        stop=(kb == LB - 1),
+                    )
+            cond_ps.append(banks)
 
         out_blocks = out.rearrange("(b p) n -> b p n", p=P)
-        for mb in range(MB):
-            result = held.tile([P, N], F32, name=f"result{mb}")
-            nc.vector.scalar_tensor_tensor(
-                result[:], scale_ps[mb][:], branch[:, mb : mb + 1], residual[mb][:], MULT, ADD
-            )
-            nc.sync.dma_start(out_blocks[mb, :, :], result[:])
+        for piece in range(PIECES):
+            h_bf = []
+            for db in range(LB):
+                activated = held.tile([P, PIECE], BF16, name=f"h_bf{piece}_{db}")
+                nc.scalar.activation(activated[:], cond_ps[piece][db][:], SILU, bias=cond_bias[:, db : db + 1])
+                h_bf.append(activated)
+            scale_ps = [psum.tile([P, PIECE], F32, name=f"scale_ps{piece}_{mb}", tag="bank") for mb in range(MB)]
+            for db in range(LB):
+                for mb in range(MB):
+                    nc.tensor.matmul(
+                        scale_ps[mb][:],
+                        cond_w2_sb[:, db, mb * P : (mb + 1) * P],
+                        h_bf[db][:],
+                        start=(db == 0),
+                        stop=(db == LB - 1),
+                    )
+            for mb in range(MB):
+                result = held.tile([P, PIECE], F32, name=f"result{piece}_{mb}")
+                nc.vector.scalar_tensor_tensor(
+                    result[:],
+                    scale_ps[mb][:],
+                    branch[:, mb : mb + 1],
+                    residual[mb][:, piece * PIECE : (piece + 1) * PIECE],
+                    MULT,
+                    ADD,
+                )
+                nc.sync.dma_start(out_blocks[mb, :, piece * PIECE : (piece + 1) * PIECE], result[:])

@@ -14,7 +14,10 @@ LB = L // P
 MB = M // P
 PIECE = S
 PIECES = N // PIECE
-PSUM_BANKS = 8
+UNITS = PIECES * LB
+BANK = 512
+SILU_LAG = 1
+COND_LAG = LB + 1
 FLOPS = 2 * L * L * N + 2 * L * M * N
 
 
@@ -22,7 +25,7 @@ def tile_conditionalflow_kernel(tc, table, emb_w, emb_b, cond_w2, cond_b2, mlp_b
     nc = tc.nc
     with (
         tc.tile_pool(name="held", bufs=1) as held,
-        tc.psum_pool(name="psum", bufs=PSUM_BANKS) as psum,
+        tc.psum_pool(name="psum", bufs=1) as psum,
     ):
         scratch = held.tile([P, 1], F32, name="scratch")
         nc.vector.memset(scratch[:], 0.0)
@@ -36,12 +39,6 @@ def tile_conditionalflow_kernel(tc, table, emb_w, emb_b, cond_w2, cond_b2, mlp_b
             window = held.tile([P, S], F32, name=f"window{kb}")
             nc.sync.dma_start(window[:], table_blocks[kb, :, :])
             windows.append(window)
-        emb_w_blocks = emb_w.rearrange("(b p) d -> b p d", p=P)
-        emb_w_sb = []
-        for kb in range(LB):
-            weights = held.tile([P, L], BF16, name=f"emb_w{kb}")
-            nc.sync.dma_start(weights[:], emb_w_blocks[kb, :, :])
-            emb_w_sb.append(weights)
         cond_bias = held.tile([P, LB], F32, name="cond_bias")
         branch = held.tile([P, MB], F32, name="branch")
         scale_bias = held.tile([P, MB], F32, name="scale_bias")
@@ -49,6 +46,13 @@ def tile_conditionalflow_kernel(tc, table, emb_w, emb_b, cond_w2, cond_b2, mlp_b
             nc.sync.dma_start(cond_bias[:], emb_b.rearrange("(b p) o -> p (b o)", p=P))
             nc.sync.dma_start(branch[:], mlp_b2.rearrange("(b p) o -> p (b o)", p=P))
             nc.sync.dma_start(scale_bias[:], cond_b2.rearrange("(b p) o -> p (b o)", p=P))
+
+        emb_w_blocks = emb_w.rearrange("(b p) d -> b p d", p=P)
+        emb_w_sb = []
+        for kb in range(LB):
+            weights = held.tile([P, L], BF16, name=f"emb_w{kb}")
+            nc.scalar.dma_start(weights[:], emb_w_blocks[kb, :, :])
+            emb_w_sb.append(weights)
 
         cond_w2_sb = held.tile([P, LB, M], BF16, name="cond_w2_sb")
         nc.gpsimd.dma_start(cond_w2_sb[:], cond_w2.rearrange("(b p) m -> p b m", p=P))
@@ -65,56 +69,61 @@ def tile_conditionalflow_kernel(tc, table, emb_w, emb_b, cond_w2, cond_b2, mlp_b
         for mb in range(MB):
             nc.vector.tensor_scalar_add(residual[mb][:], residual[mb][:], shift[:, mb : mb + 1])
 
-        cond_ps = []
-        for piece in range(PIECES):
-            piece_offsets = offsets[:, piece * PIECE // 16 : (piece + 1) * PIECE // 16]
-            picked = []
-            for kb in range(LB):
-                columns = held.tile([P, PIECE], F32, name=f"picked{piece}_{kb}")
-                nc.scalar.activation(columns[:], windows[kb][:].indirect(piece_offsets), COPY)
-                picked.append(columns)
-            e_bf = []
-            for kb in range(LB):
-                activated = held.tile([P, PIECE], BF16, name=f"e_bf{piece}_{kb}")
-                nc.scalar.activation(activated[:], picked[kb][:], SILU)
-                e_bf.append(activated)
-            banks = [psum.tile([P, PIECE], F32, name=f"cond_ps{piece}_{db}", tag="bank") for db in range(LB)]
-            for kb in range(LB):
+        banks = [
+            [psum.tile([P, BANK], F32, name=f"bank{piece}_{db}") for db in range(LB)] for piece in range(PIECES)
+        ]
+        cond_ps = [[banks[piece][db][:, 0:PIECE] for db in range(LB)] for piece in range(PIECES)]
+        scale_ps = [[banks[0][piece * MB + mb][:, PIECE:BANK] for mb in range(MB)] for piece in range(PIECES)]
+
+        out_blocks = out.rearrange("(b p) n -> b p n", p=P)
+        picked = {}
+        for step in range(UNITS + COND_LAG):
+            if step < UNITS:
+                piece, kb = divmod(step, LB)
+                columns = held.tile([P, PIECE], F32, name=f"picked{step}")
+                nc.scalar.activation(
+                    columns[:],
+                    windows[kb][:].indirect(offsets[:, piece * PIECE // 16 : (piece + 1) * PIECE // 16]),
+                    COPY,
+                )
+                picked[step] = columns
+
+            unit = step - SILU_LAG
+            if 0 <= unit < UNITS:
+                piece, kb = divmod(unit, LB)
+                e_bf = held.tile([P, PIECE], BF16, name=f"e_bf{unit}")
+                nc.scalar.activation(e_bf[:], picked[unit][:], SILU)
                 for db in range(LB):
                     nc.tensor.matmul(
-                        banks[db][:],
+                        cond_ps[piece][db],
                         emb_w_sb[kb][:, db * P : (db + 1) * P],
-                        e_bf[kb][:],
+                        e_bf[:],
                         start=(kb == 0),
                         stop=(kb == LB - 1),
                     )
-            cond_ps.append(banks)
 
-        out_blocks = out.rearrange("(b p) n -> b p n", p=P)
-        for piece in range(PIECES):
-            h_bf = []
-            for db in range(LB):
-                activated = held.tile([P, PIECE], BF16, name=f"h_bf{piece}_{db}")
-                nc.scalar.activation(activated[:], cond_ps[piece][db][:], SILU, bias=cond_bias[:, db : db + 1])
-                h_bf.append(activated)
-            scale_ps = [psum.tile([P, PIECE], F32, name=f"scale_ps{piece}_{mb}", tag="bank") for mb in range(MB)]
-            for db in range(LB):
+            unit = step - COND_LAG
+            if 0 <= unit:
+                piece, db = divmod(unit, LB)
+                h_bf = held.tile([P, PIECE], BF16, name=f"h_bf{unit}")
+                nc.scalar.activation(h_bf[:], cond_ps[piece][db], SILU, bias=cond_bias[:, db : db + 1])
                 for mb in range(MB):
                     nc.tensor.matmul(
-                        scale_ps[mb][:],
+                        scale_ps[piece][mb],
                         cond_w2_sb[:, db, mb * P : (mb + 1) * P],
-                        h_bf[db][:],
+                        h_bf[:],
                         start=(db == 0),
                         stop=(db == LB - 1),
                     )
-            for mb in range(MB):
-                result = held.tile([P, PIECE], F32, name=f"result{piece}_{mb}")
-                nc.vector.scalar_tensor_tensor(
-                    result[:],
-                    scale_ps[mb][:],
-                    branch[:, mb : mb + 1],
-                    residual[mb][:, piece * PIECE : (piece + 1) * PIECE],
-                    MULT,
-                    ADD,
-                )
-                nc.sync.dma_start(out_blocks[mb, :, piece * PIECE : (piece + 1) * PIECE], result[:])
+                if db == LB - 1:
+                    for mb in range(MB):
+                        result = held.tile([P, PIECE], F32, name=f"result{piece}_{mb}")
+                        nc.vector.scalar_tensor_tensor(
+                            result[:],
+                            scale_ps[piece][mb],
+                            branch[:, mb : mb + 1],
+                            residual[mb][:, piece * PIECE : (piece + 1) * PIECE],
+                            MULT,
+                            ADD,
+                        )
+                        nc.sync.dma_start(out_blocks[mb, :, piece * PIECE : (piece + 1) * PIECE], result[:])

@@ -17,7 +17,7 @@ PIECES = N // PIECE
 UNITS = PIECES * LB
 BANK = 512
 SILU_LAG = 1
-COND_LAG = LB + 1
+COND_LAG = LB + 2
 FLOPS = 2 * L * L * N + 2 * L * M * N
 
 

@@ -77,6 +77,29 @@ def tile_conditionalflow_kernel(tc, table, emb_w, emb_b, cond_w2, cond_b2, mlp_b
 
         out_blocks = out.rearrange("(b p) n -> b p n", p=P)
         picked = {}
+        hidden = {}
+
+        def project(piece, mb, db):
+            nc.tensor.matmul(
+                scale_ps[piece][mb],
+                cond_w2_sb[:, db, mb * P : (mb + 1) * P],
+                hidden[piece, db][:],
+                start=(db == 0),
+                stop=(db == LB - 1),
+            )
+
+        def finish(piece, mb):
+            result = held.tile([P, PIECE], F32, name=f"result{piece}_{mb}")
+            nc.vector.scalar_tensor_tensor(
+                result[:],
+                scale_ps[piece][mb],
+                branch[:, mb : mb + 1],
+                residual[mb][:, piece * PIECE : (piece + 1) * PIECE],
+                MULT,
+                ADD,
+            )
+            nc.sync.dma_start(out_blocks[mb, :, piece * PIECE : (piece + 1) * PIECE], result[:])
+
         for step in range(UNITS + COND_LAG):
             if step < UNITS:
                 piece, kb = divmod(step, LB)
@@ -107,23 +130,17 @@ def tile_conditionalflow_kernel(tc, table, emb_w, emb_b, cond_w2, cond_b2, mlp_b
                 piece, db = divmod(unit, LB)
                 h_bf = held.tile([P, PIECE], BF16, name=f"h_bf{unit}")
                 nc.scalar.activation(h_bf[:], cond_ps[piece][db], SILU, bias=cond_bias[:, db : db + 1])
-                for mb in range(MB):
-                    nc.tensor.matmul(
-                        scale_ps[piece][mb],
-                        cond_w2_sb[:, db, mb * P : (mb + 1) * P],
-                        h_bf[:],
-                        start=(db == 0),
-                        stop=(db == LB - 1),
-                    )
-                if db == LB - 1:
+                hidden[piece, db] = h_bf
+                if piece < PIECES - 1:
                     for mb in range(MB):
-                        result = held.tile([P, PIECE], F32, name=f"result{piece}_{mb}")
-                        nc.vector.scalar_tensor_tensor(
-                            result[:],
-                            scale_ps[piece][mb],
-                            branch[:, mb : mb + 1],
-                            residual[mb][:, piece * PIECE : (piece + 1) * PIECE],
-                            MULT,
-                            ADD,
-                        )
-                        nc.sync.dma_start(out_blocks[mb, :, piece * PIECE : (piece + 1) * PIECE], result[:])
+                        project(piece, mb, db)
+                        if db == LB - 1:
+                            finish(piece, mb)
+                elif db == 0:
+                    for mb in range(MB):
+                        project(piece, mb, db)
+                elif db == LB - 1:
+                    for mb in range(MB):
+                        for later_db in range(1, LB):
+                            project(piece, mb, later_db)
+                        finish(piece, mb)

@@ -40,12 +40,8 @@ def tile_conditionalflow_kernel(tc, table, emb_w, emb_b, cond_w2, cond_b2, mlp_b
             nc.sync.dma_start(window[:], table_blocks[kb, :, :])
             windows.append(window)
         cond_bias = held.tile([P, LB], F32, name="cond_bias")
-        branch = held.tile([P, MB], F32, name="branch")
-        scale_bias = held.tile([P, MB], F32, name="scale_bias")
         with nc.allow_non_contiguous_dma(reason="a bias vector, one value to a partition"):
             nc.sync.dma_start(cond_bias[:], emb_b.rearrange("(b p) o -> p (b o)", p=P))
-            nc.sync.dma_start(branch[:], mlp_b2.rearrange("(b p) o -> p (b o)", p=P))
-            nc.sync.dma_start(scale_bias[:], cond_b2.rearrange("(b p) o -> p (b o)", p=P))
 
         emb_w_blocks = emb_w.rearrange("(b p) d -> b p d", p=P)
         emb_w_sb = []
@@ -62,6 +58,11 @@ def tile_conditionalflow_kernel(tc, table, emb_w, emb_b, cond_w2, cond_b2, mlp_b
             x_sb = held.tile([P, N], F32, name=f"x{mb}")
             nc.gpsimd.dma_start(x_sb[:], x_blocks[mb, :, :])
             residual.append(x_sb)
+        branch = held.tile([P, MB], F32, name="branch")
+        scale_bias = held.tile([P, MB], F32, name="scale_bias")
+        with nc.allow_non_contiguous_dma(reason="a bias vector, one value to a partition"):
+            nc.gpsimd.dma_start(branch[:], mlp_b2.rearrange("(b p) o -> p (b o)", p=P))
+            nc.gpsimd.dma_start(scale_bias[:], cond_b2.rearrange("(b p) o -> p (b o)", p=P))
 
         nc.vector.tensor_scalar_add(cond_bias[:, LB // 2 :], cond_bias[:, LB // 2 :], 1.0)
         shift = held.tile([P, MB], F32, name="shift")

@@ -16,6 +16,7 @@ PIECE = S
 PIECES = N // PIECE
 UNITS = PIECES * LB
 BANK = 512
+BLOCK32 = 8
 SILU_LAG = 1
 COND_LAG = LB + 2
 FLOPS = 2 * L * L * N + 2 * L * M * N
@@ -58,17 +59,8 @@ def tile_conditionalflow_kernel(tc, table, emb_w, emb_b, cond_w2, cond_b2, mlp_b
             x_sb = held.tile([P, N], F32, name=f"x{mb}")
             nc.gpsimd.dma_start(x_sb[:], x_blocks[mb, :, :])
             residual.append(x_sb)
-        branch = held.tile([P, MB], F32, name="branch")
-        scale_bias = held.tile([P, MB], F32, name="scale_bias")
-        with nc.allow_non_contiguous_dma(reason="a bias vector, one value to a partition"):
-            nc.gpsimd.dma_start(branch[:], mlp_b2.rearrange("(b p) o -> p (b o)", p=P))
-            nc.gpsimd.dma_start(scale_bias[:], cond_b2.rearrange("(b p) o -> p (b o)", p=P))
 
         nc.vector.tensor_scalar_add(cond_bias[:, LB // 2 :], cond_bias[:, LB // 2 :], 1.0)
-        shift = held.tile([P, MB], F32, name="shift")
-        nc.vector.scalar_tensor_tensor(shift[:], scale_bias[:], 1.0, branch[:], ADD, MULT)
-        for mb in range(MB):
-            nc.vector.tensor_scalar_add(residual[mb][:], residual[mb][:], shift[:, mb : mb + 1])
 
         banks = [
             [psum.tile([P, BANK], F32, name=f"bank{piece}_{db}") for db in range(LB)] for piece in range(PIECES)
@@ -79,6 +71,19 @@ def tile_conditionalflow_kernel(tc, table, emb_w, emb_b, cond_w2, cond_b2, mlp_b
         out_blocks = out.rearrange("(b p) n -> b p n", p=P)
         picked = {}
         hidden = {}
+
+        def load_output_vectors():
+            vectors = held.tile([P, 2 * BLOCK32], F32, name="vectors", tag="picked0")
+            branch = vectors[:, 0:MB]
+            scale_bias = vectors[:, BLOCK32 : BLOCK32 + MB]
+            with nc.allow_non_contiguous_dma(reason="a bias vector, one value to a partition"):
+                nc.sync.dma_start(branch, mlp_b2.rearrange("(b p) o -> p (b o)", p=P))
+                nc.sync.dma_start(scale_bias, cond_b2.rearrange("(b p) o -> p (b o)", p=P))
+            shift = held.tile([P, MB], F32, name="shift")
+            nc.vector.scalar_tensor_tensor(shift[:], scale_bias, 1.0, branch, ADD, MULT)
+            for mb in range(MB):
+                nc.vector.tensor_scalar_add(residual[mb][:], residual[mb][:], shift[:, mb : mb + 1])
+            return branch
 
         def project(piece, mb, db):
             nc.tensor.matmul(
@@ -117,6 +122,8 @@ def tile_conditionalflow_kernel(tc, table, emb_w, emb_b, cond_w2, cond_b2, mlp_b
                 piece, kb = divmod(unit, LB)
                 e_bf = held.tile([P, PIECE], BF16, name=f"e_bf{unit}")
                 nc.scalar.activation(e_bf[:], picked[unit][:], SILU)
+                if unit == 0:
+                    branch = load_output_vectors()
                 for db in range(LB):
                     nc.tensor.matmul(
                         cond_ps[piece][db],

@@ -42,7 +42,7 @@ def tile_conditionalflow_kernel(tc, table, emb_w, emb_b, cond_w2, cond_b2, mlp_b
             windows.append(window)
         cond_bias = held.tile([P, LB], F32, name="cond_bias")
         with nc.allow_non_contiguous_dma(reason="a bias vector, one value to a partition"):
-            nc.sync.dma_start(cond_bias[:], emb_b.rearrange("(b p) o -> p (b o)", p=P))
+            nc.sync.dma_start(cond_bias[:], emb_b.rearrange("(p b) o -> p (b o)", p=P))
 
         emb_w_blocks = emb_w.rearrange("(b p) d -> b p d", p=P)
         emb_w_sb = []
@@ -52,15 +52,11 @@ def tile_conditionalflow_kernel(tc, table, emb_w, emb_b, cond_w2, cond_b2, mlp_b
             emb_w_sb.append(weights)
 
         cond_w2_sb = held.tile([P, LB, M], BF16, name="cond_w2_sb")
-        nc.gpsimd.dma_start(cond_w2_sb[:], cond_w2.rearrange("(b p) m -> p b m", p=P))
-        x_blocks = x.rearrange("(b p) n -> b p n", p=P)
-        residual = []
-        for mb in range(MB):
-            x_sb = held.tile([P, N], F32, name=f"x{mb}")
-            nc.gpsimd.dma_start(x_sb[:], x_blocks[mb, :, :])
-            residual.append(x_sb)
+        nc.gpsimd.dma_start(cond_w2_sb[:], cond_w2.rearrange("(p b) m -> p b m", p=P))
+        residual = held.tile([P, MB, N], F32, name="residual")
+        nc.gpsimd.dma_start(residual[:], x.rearrange("(p b) n -> p b n", p=P))
 
-        nc.vector.tensor_scalar_add(cond_bias[:, LB // 2 :], cond_bias[:, LB // 2 :], 1.0)
+        nc.vector.tensor_scalar_add(cond_bias[P // 2 :, :], cond_bias[P // 2 :, :], 1.0)
 
         banks = [
             [psum.tile([P, BANK], F32, name=f"bank{piece}_{db}") for db in range(LB)] for piece in range(PIECES)
@@ -68,7 +64,7 @@ def tile_conditionalflow_kernel(tc, table, emb_w, emb_b, cond_w2, cond_b2, mlp_b
         cond_ps = [[banks[piece][db][:, 0:PIECE] for db in range(LB)] for piece in range(PIECES)]
         scale_ps = [[banks[0][piece * MB + mb][:, PIECE:BANK] for mb in range(MB)] for piece in range(PIECES)]
 
-        out_blocks = out.rearrange("(b p) n -> b p n", p=P)
+        out_blocks = out.rearrange("(p b) n -> b p n", p=P)
         picked = {}
         hidden = {}
 
@@ -77,18 +73,18 @@ def tile_conditionalflow_kernel(tc, table, emb_w, emb_b, cond_w2, cond_b2, mlp_b
             branch = vectors[:, 0:MB]
             scale_bias = vectors[:, BLOCK32 : BLOCK32 + MB]
             with nc.allow_non_contiguous_dma(reason="a bias vector, one value to a partition"):
-                nc.sync.dma_start(branch, mlp_b2.rearrange("(b p) o -> p (b o)", p=P))
-                nc.sync.dma_start(scale_bias, cond_b2.rearrange("(b p) o -> p (b o)", p=P))
+                nc.sync.dma_start(branch, mlp_b2.rearrange("(p b) o -> p (b o)", p=P))
+                nc.sync.dma_start(scale_bias, cond_b2.rearrange("(p b) o -> p (b o)", p=P))
             shift = held.tile([P, MB], F32, name="shift")
             nc.vector.scalar_tensor_tensor(shift[:], scale_bias, 1.0, branch, ADD, MULT)
             for mb in range(MB):
-                nc.vector.tensor_scalar_add(residual[mb][:], residual[mb][:], shift[:, mb : mb + 1])
+                nc.vector.tensor_scalar_add(residual[:, mb, :], residual[:, mb, :], shift[:, mb : mb + 1])
             return branch
 
         def project(piece, mb, db):
             nc.tensor.matmul(
                 scale_ps[piece][mb],
-                cond_w2_sb[:, db, mb * P : (mb + 1) * P],
+                cond_w2_sb[:, db, mb::MB],
                 hidden[piece, db][:],
                 start=(db == 0),
                 stop=(db == LB - 1),
@@ -100,7 +96,7 @@ def tile_conditionalflow_kernel(tc, table, emb_w, emb_b, cond_w2, cond_b2, mlp_b
                 result[:],
                 scale_ps[piece][mb],
                 branch[:, mb : mb + 1],
-                residual[mb][:, piece * PIECE : (piece + 1) * PIECE],
+                residual[:, mb, piece * PIECE : (piece + 1) * PIECE],
                 MULT,
                 ADD,
             )
@@ -127,7 +123,7 @@ def tile_conditionalflow_kernel(tc, table, emb_w, emb_b, cond_w2, cond_b2, mlp_b
                 for db in range(LB):
                     nc.tensor.matmul(
                         cond_ps[piece][db],
-                        emb_w_sb[kb][:, db * P : (db + 1) * P],
+                        emb_w_sb[kb][:, db::LB],
                         e_bf[:],
                         start=(kb == 0),
                         stop=(kb == LB - 1),

@@ -53,8 +53,6 @@ def tile_conditionalflow_kernel(tc, table, emb_w, emb_b, cond_w2, cond_b2, mlp_b
 
         cond_w2_sb = held.tile([P, LB, M], BF16, name="cond_w2_sb")
         nc.gpsimd.dma_start(cond_w2_sb[:], cond_w2.rearrange("(p b) m -> p b m", p=P))
-        residual = held.tile([P, MB, N], F32, name="residual")
-        nc.gpsimd.dma_start(residual[:], x.rearrange("(p b) n -> p b n", p=P))
 
         nc.vector.tensor_scalar_add(cond_bias[P // 2 :, :], cond_bias[P // 2 :, :], 1.0)
 
@@ -68,7 +66,9 @@ def tile_conditionalflow_kernel(tc, table, emb_w, emb_b, cond_w2, cond_b2, mlp_b
         picked = {}
         hidden = {}
 
-        def load_output_vectors():
+        def load_output_operands():
+            residual = held.tile([P, MB, N], F32, name="residual", tag="picked1")
+            nc.gpsimd.dma_start(residual[:], x.rearrange("(p b) n -> p b n", p=P))
             vectors = held.tile([P, 2 * BLOCK32], F32, name="vectors", tag="picked0")
             branch = vectors[:, 0:MB]
             scale_bias = vectors[:, BLOCK32 : BLOCK32 + MB]
@@ -79,7 +79,7 @@ def tile_conditionalflow_kernel(tc, table, emb_w, emb_b, cond_w2, cond_b2, mlp_b
             nc.vector.scalar_tensor_tensor(shift[:], scale_bias, 1.0, branch, ADD, MULT)
             for mb in range(MB):
                 nc.vector.tensor_scalar_add(residual[:, mb, :], residual[:, mb, :], shift[:, mb : mb + 1])
-            return branch
+            return branch, residual
 
         def project(piece, mb, db):
             nc.tensor.matmul(
@@ -118,8 +118,8 @@ def tile_conditionalflow_kernel(tc, table, emb_w, emb_b, cond_w2, cond_b2, mlp_b
                 piece, kb = divmod(unit, LB)
                 e_bf = held.tile([P, PIECE], BF16, name=f"e_bf{unit}")
                 nc.scalar.activation(e_bf[:], picked[unit][:], SILU)
-                if unit == 0:
-                    branch = load_output_vectors()
+                if unit == 1:
+                    branch, residual = load_output_operands()
                 for db in range(LB):
                     nc.tensor.matmul(
                         cond_ps[piece][db],

@@ -18,6 +18,7 @@ UNITS = PIECES * LB
 BANK = 512
 BLOCK32 = 8
 SILU_LAG = 1
+LAST_SILU_STEP = UNITS - 1 + SILU_LAG
 COND_LAG = LB + 2
 FLOPS = 2 * L * L * N + 2 * L * M * N
 
@@ -130,21 +131,28 @@ def tile_conditionalflow_kernel(tc, table, emb_w, emb_b, cond_w2, cond_b2, mlp_b
                     )
 
             unit = step - COND_LAG
-            if 0 <= unit:
+            if 0 <= unit < UNITS:
                 piece, db = divmod(unit, LB)
                 h_bf = held.tile([P, PIECE], BF16, name=f"h_bf{unit}")
                 nc.scalar.activation(h_bf[:], cond_ps[piece][db], SILU, bias=cond_bias[:, db : db + 1])
                 hidden[piece, db] = h_bf
-                if piece < PIECES - 1:
-                    for mb in range(MB):
-                        project(piece, mb, db)
-                        if db == LB - 1:
-                            finish(piece, mb)
-                elif db == 0:
-                    for mb in range(MB):
-                        project(piece, mb, db)
-                elif db == LB - 1:
-                    for mb in range(MB):
-                        for later_db in range(1, LB):
-                            project(piece, mb, later_db)
+
+            if step == LAST_SILU_STEP - 1:
+                projected = []
+            elif step == LAST_SILU_STEP:
+                projected = [unit - 1, unit]
+            else:
+                projected = [unit]
+            for unit in projected:
+                piece, db = divmod(unit, LB)
+                if unit < 0 or (piece == PIECES - 1 and db > 0):
+                    continue
+                for mb in range(MB):
+                    project(piece, mb, db)
+                    if db == LB - 1:
                         finish(piece, mb)
+            if step == UNITS - 1 + COND_LAG:
+                for mb in range(MB):
+                    for later_db in range(1, LB):
+                        project(PIECES - 1, mb, later_db)
+                    finish(PIECES - 1, mb)

@@ -33,14 +33,15 @@ def tile_conditionalflow_kernel(tc, table, emb_w, emb_b, cond_w2, cond_b2, mlp_b
         nc.vector.memset(scratch[:], 0.0)
         nc.scalar.activation(scratch[:], scratch[:], SILU)
 
-        offsets = held.tile([P, N // 16], U16, name="offsets")
-        nc.sync.dma_start(offsets[:], offs)
         table_blocks = table.rearrange("(b p) s -> b p s", p=P)
         windows = []
         for kb in range(LB):
             window = held.tile([P, S], F32, name=f"window{kb}")
             nc.sync.dma_start(window[:], table_blocks[kb, :, :])
             windows.append(window)
+            if kb == 0:
+                offsets = held.tile([P, N // 16], U16, name="offsets")
+                nc.sync.dma_start(offsets[:], offs)
         cond_bias = held.tile([P, LB], F32, name="cond_bias")
         with nc.allow_non_contiguous_dma(reason="a bias vector, one value to a partition"):
             nc.sync.dma_start(cond_bias[:], emb_b.rearrange("(p b) o -> p (b o)", p=P))

@@ -87,7 +87,7 @@ def tile_conditionalflow_kernel(tc, table, emb_w, emb_b, cond_w2, cond_b2, mlp_b
             nc.tensor.matmul(
                 scale_ps[piece][mb],
                 cond_w2_sb[:, db, mb::MB],
-                hidden[piece, db][:],
+                hidden[piece, db],
                 start=(db == 0),
                 stop=(db == LB - 1),
             )
@@ -131,27 +131,30 @@ def tile_conditionalflow_kernel(tc, table, emb_w, emb_b, cond_w2, cond_b2, mlp_b
                         stop=(kb == LB - 1),
                     )
 
+            if step == LB - 1 + SILU_LAG:
+                biased = held.tile([P, LB - 1, PIECE], F32, name="biased")
+                for db in range(1, LB):
+                    nc.vector.tensor_scalar_add(biased[:, db - 1, :], cond_ps[0][db], cond_bias[:, db : db + 1])
+
             unit = step - COND_LAG
-            if 0 <= unit < UNITS:
+            if unit == 0 or LB <= unit:
                 piece, db = divmod(unit, LB)
                 h_bf = held.tile([P, PIECE], BF16, name=f"h_bf{unit}")
                 nc.scalar.activation(h_bf[:], cond_ps[piece][db], SILU, bias=cond_bias[:, db : db + 1])
-                hidden[piece, db] = h_bf
-
-            if step == LAST_SILU_STEP - 1:
-                projected = []
+                hidden[piece, db] = h_bf[:]
+                if db == 0:
+                    for mb in range(MB):
+                        project(piece, mb, db)
             elif step == LAST_SILU_STEP:
-                projected = [unit - 1, unit]
-            else:
-                projected = [unit]
-            for unit in projected:
-                piece, db = divmod(unit, LB)
-                if unit < 0 or (piece == PIECES - 1 and db > 0):
-                    continue
+                h_wide = held.tile([P, LB - 1, PIECE], BF16, name="h_wide")
+                nc.scalar.activation(h_wide[:], biased[:], SILU)
+                for db in range(1, LB):
+                    hidden[0, db] = h_wide[:, db - 1, :]
+                    for mb in range(MB):
+                        project(0, mb, db)
                 for mb in range(MB):
-                    project(piece, mb, db)
-                    if db == LB - 1:
-                        finish(piece, mb)
+                    finish(0, mb)
+
             if step == UNITS - 1 + COND_LAG:
                 for mb in range(MB):
                     for later_db in range(1, LB):

import concourse.mybir as mybir

F32 = mybir.dt.float32
BF16 = mybir.dt.bfloat16
U16 = mybir.dt.uint16
COPY = mybir.ActivationFunctionType.Copy
SILU = mybir.ActivationFunctionType.Silu
ADD = mybir.AluOpType.add
MULT = mybir.AluOpType.mult

P = 128
L, S, M, N = 512, 256, 256, 512
LB = L // P
MB = M // P
PIECE = S
PIECES = N // PIECE
UNITS = PIECES * LB
BANK = 512
BLOCK32 = 8
SILU_LAG = 1
LAST_SILU_STEP = UNITS - 1 + SILU_LAG
COND_LAG = LB + 2
FLOPS = 2 * L * L * N + 2 * L * M * N


def tile_conditionalflow_kernel(tc, table, emb_w, emb_b, cond_w2, cond_b2, mlp_b2, x, offs, out):
    nc = tc.nc
    with (
        tc.tile_pool(name="held", bufs=1) as held,
        tc.psum_pool(name="psum", bufs=1) as psum,
    ):
        scratch = held.tile([P, 1], F32, name="scratch")
        nc.vector.memset(scratch[:], 0.0)
        nc.scalar.activation(scratch[:], scratch[:], SILU)

        table_blocks = table.rearrange("(b p) s -> b p s", p=P)
        windows = []
        for kb in range(LB):
            window = held.tile([P, S], F32, name=f"window{kb}")
            nc.sync.dma_start(window[:], table_blocks[kb, :, :])
            windows.append(window)
            if kb == 0:
                offsets = held.tile([P, N // 16], U16, name="offsets")
                nc.sync.dma_start(offsets[:], offs)
        cond_bias = held.tile([P, LB], F32, name="cond_bias")
        with nc.allow_non_contiguous_dma(reason="a bias vector, one value to a partition"):
            nc.sync.dma_start(cond_bias[:], emb_b.rearrange("(p b) o -> p (b o)", p=P))

        emb_w_blocks = emb_w.rearrange("(b p) d -> b p d", p=P)
        emb_w_sb = []
        for kb in range(LB):
            weights = held.tile([P, L], BF16, name=f"emb_w{kb}")
            nc.scalar.dma_start(weights[:], emb_w_blocks[kb, :, :])
            emb_w_sb.append(weights)

        cond_w2_sb = held.tile([P, LB, M], BF16, name="cond_w2_sb")
        nc.gpsimd.dma_start(cond_w2_sb[:], cond_w2.rearrange("(p b) m -> p b m", p=P))

        nc.vector.tensor_scalar_add(cond_bias[P // 2 :, :], cond_bias[P // 2 :, :], 1.0)

        banks = [
            [psum.tile([P, BANK], F32, name=f"bank{piece}_{db}") for db in range(LB)] for piece in range(PIECES)
        ]
        cond_ps = [[banks[piece][db][:, 0:PIECE] for db in range(LB)] for piece in range(PIECES)]
        scale_ps = [[banks[0][piece * MB + mb][:, PIECE:BANK] for mb in range(MB)] for piece in range(PIECES)]

        out_blocks = out.rearrange("(p b) n -> b p n", p=P)
        picked = {}
        hidden = {}

        def load_output_operands():
            residual = held.tile([P, MB, N], F32, name="residual", tag="picked1")
            nc.gpsimd.dma_start(residual[:], x.rearrange("(p b) n -> p b n", p=P))
            vectors = held.tile([P, 2 * BLOCK32], F32, name="vectors", tag="picked0")
            branch = vectors[:, 0:MB]
            scale_bias = vectors[:, BLOCK32 : BLOCK32 + MB]
            with nc.allow_non_contiguous_dma(reason="a bias vector, one value to a partition"):
                nc.sync.dma_start(branch, mlp_b2.rearrange("(p b) o -> p (b o)", p=P))
                nc.sync.dma_start(scale_bias, cond_b2.rearrange("(p b) o -> p (b o)", p=P))
            shift = held.tile([P, MB], F32, name="shift")
            nc.vector.scalar_tensor_tensor(shift[:], scale_bias, 1.0, branch, ADD, MULT)
            for mb in range(MB):
                nc.vector.tensor_scalar_add(residual[:, mb, :], residual[:, mb, :], shift[:, mb : mb + 1])
            return branch, residual

        def project(piece, mb, db):
            nc.tensor.matmul(
                scale_ps[piece][mb],
                cond_w2_sb[:, db, mb::MB],
                hidden[piece, db],
                start=(db == 0),
                stop=(db == LB - 1),
            )

        def finish(piece, mb):
            result = held.tile([P, PIECE], F32, name=f"result{piece}_{mb}")
            nc.vector.scalar_tensor_tensor(
                result[:],
                scale_ps[piece][mb],
                branch[:, mb : mb + 1],
                residual[:, mb, piece * PIECE : (piece + 1) * PIECE],
                MULT,
                ADD,
            )
            nc.sync.dma_start(out_blocks[mb, :, piece * PIECE : (piece + 1) * PIECE], result[:])

        for step in range(UNITS + COND_LAG):
            if step < UNITS:
                piece, kb = divmod(step, LB)
                columns = held.tile([P, PIECE], F32, name=f"picked{step}")
                nc.scalar.activation(
                    columns[:],
                    windows[kb][:].indirect(offsets[:, piece * PIECE // 16 : (piece + 1) * PIECE // 16]),
                    COPY,
                )
                picked[step] = columns

            unit = step - SILU_LAG
            if 0 <= unit < UNITS:
                piece, kb = divmod(unit, LB)
                e_bf = held.tile([P, PIECE], BF16, name=f"e_bf{unit}")
                nc.scalar.activation(e_bf[:], picked[unit][:], SILU)
                if unit == 1:
                    branch, residual = load_output_operands()
                for db in range(LB):
                    nc.tensor.matmul(
                        cond_ps[piece][db],
                        emb_w_sb[kb][:, db::LB],
                        e_bf[:],
                        start=(kb == 0),
                        stop=(kb == LB - 1),
                    )

            if step == LB - 1 + SILU_LAG:
                biased = held.tile([P, LB - 1, PIECE], F32, name="biased")
                for db in range(1, LB):
                    nc.vector.tensor_scalar_add(biased[:, db - 1, :], cond_ps[0][db], cond_bias[:, db : db + 1])

            unit = step - COND_LAG
            if unit == 0 or LB <= unit:
                piece, db = divmod(unit, LB)
                h_bf = held.tile([P, PIECE], BF16, name=f"h_bf{unit}")
                nc.scalar.activation(h_bf[:], cond_ps[piece][db], SILU, bias=cond_bias[:, db : db + 1])
                hidden[piece, db] = h_bf[:]
                if db == 0:
                    for mb in range(MB):
                        project(piece, mb, db)
            elif step == LAST_SILU_STEP:
                h_wide = held.tile([P, LB - 1, PIECE], BF16, name="h_wide")
                nc.scalar.activation(h_wide[:], biased[:], SILU)
                for db in range(1, LB):
                    hidden[0, db] = h_wide[:, db - 1, :]
                    for mb in range(MB):
                        project(0, mb, db)
                for mb in range(MB):
                    finish(0, mb)

            if step == UNITS - 1 + COND_LAG:
                for mb in range(MB):
                    for later_db in range(1, LB):
                        project(PIECES - 1, mb, later_db)
                    finish(PIECES - 1, mb)
